import numpy as np
import ml_dtypes


def mxq(x, axis, fmt="e4m3"):
    dtype, down = {"e4m3": (ml_dtypes.float8_e4m3fn, 7), "e5m2": (ml_dtypes.float8_e5m2, 14)}[fmt]
    v = np.moveaxis(np.asarray(x, np.float32).astype(ml_dtypes.bfloat16).astype(np.float64), axis, -1)
    blocks = v.reshape(v.shape[:-1] + (-1, 32))
    amax = np.abs(blocks).max(-1, keepdims=True)
    byte = np.maximum(np.where(amax > 0, np.frexp(amax)[1] - 1 + 127, 0) - down, 1)
    scale = np.exp2(byte - 127.0)
    codes = (blocks / scale).astype(np.float32).astype(dtype).astype(np.float64)
    return np.moveaxis((codes * scale).reshape(v.shape), -1, axis)


WIDE = False


def mx_kscale(k):
    if not WIDE:
        return np.ones(k)
    levels = np.array([10, -10, 5, -5, 0])
    a = np.random.permutation(np.resize(levels, k // 512 * 4)).reshape(k // 512, 4)
    idx = np.arange(k)
    return np.exp2(a[idx // 512, idx % 128 // 32])


BF16 = ml_dtypes.bfloat16


def bf(x):
    return np.asarray(x, np.float32).astype(BF16)


def f64(x):
    return np.asarray(x).astype(np.float64)


B, R, C, H, DH = 16, 8, 1536, 12, 128
T = R * R
E = H * DH
EPS = 2.0 ** -23


def rmsnorm(v):
    return v * (1.0 / np.sqrt(np.mean(np.square(v), axis=-1, keepdims=True) + EPS))


def setup_inputs():
    s = mx_kscale(C)
    return {"x": bf(np.random.standard_normal((B, T, C)) * s),
            "Wq": bf(np.random.standard_normal((C, E)) / np.sqrt(C) / s[:, None]),
            "Wk": bf(np.random.standard_normal((C, E)) / np.sqrt(C) / s[:, None])}


def reference(x, Wq, Wk):
    xq = mxq(f64(x), 2, "e4m3")

    def proj(W):
        return (xq @ mxq(f64(W), 0, "e4m3")).reshape(B, T, H, DH).transpose(0, 2, 1, 3)

    return rmsnorm(proj(Wq)), rmsnorm(proj(Wk))

@@ -1,0 +1,211 @@
+from contextlib import ExitStack
+
+import concourse.mybir as mybir
+from concourse.masks import make_identity
+
+F32 = mybir.dt.float32
+BF16 = mybir.dt.bfloat16
+U32 = mybir.dt.uint32
+U8 = mybir.dt.uint8
+FP8X4 = mybir.dt.float8_e4m3fn_x4
+ACT = mybir.ActivationFunctionType
+ALU = mybir.AluOpType
+
+P = 128
+PACK = 4
+K_PASS = P * PACK
+BOARDS, SQUARES, C, HEADS, DH = 16, 64, 1536, 12, 128
+TOKENS = BOARDS * SQUARES
+TOKEN_TILES = TOKENS // P
+PASSES = C // K_PASS
+BLOCK = 512
+BLOCK_HEADS = BLOCK // DH
+BLOCKS_PER_WEIGHT = HEADS * DH // BLOCK
+EPS = 2.0 ** -23
+SCALAR_SCALES_EVERY = 3
+STORE_TILES = 4
+SCALE_LAG = 2
+
+FLOPS = 2 * TOKENS * C * 2 * HEADS * DH
+
+
+def tile_pieceroutedattention_pa_kernel(tc, x, Wq, Wk, out_0, out_1):
+    nc = tc.nc
+    blocks = [(w, out, b) for (w, out) in ((Wq, out_0), (Wk, out_1)) for b in range(BLOCKS_PER_WEIGHT)]
+
+    with ExitStack() as ctx:
+        const = ctx.enter_context(tc.tile_pool(name="const", bufs=1))
+        x_raw_pool = ctx.enter_context(tc.tile_pool(name="x_raw", bufs=TOKEN_TILES))
+        x_stage = ctx.enter_context(tc.tile_pool(name="x_stage", bufs=4))
+        w_raw_pool = ctx.enter_context(tc.tile_pool(name="w_raw", bufs=len(blocks) * PASSES))
+        w_stage = ctx.enter_context(tc.tile_pool(name="w_stage", bufs=PASSES))
+        w_mx = ctx.enter_context(tc.tile_pool(name="w_mx", bufs=2))
+        norm = ctx.enter_context(tc.tile_pool(name="norm", bufs=8))
+        squares = ctx.enter_context(tc.tile_pool(name="squares", bufs=4))
+        results = ctx.enter_context(tc.tile_pool(name="results", bufs=3))
+        psum = ctx.enter_context(tc.psum_pool(name="psum", bufs=8))
+
+        ident = const.tile([P, P], F32)
+        make_identity(nc, ident[:])
+
+        def load_block(w, b):
+            pieces = []
+            for g in range(PASSES):
+                w_raw = w_raw_pool.tile([P, PACK, BLOCK], BF16)
+                for u in range(2):
+                    k0 = K_PASS * g + 2 * P * u
+                    nc.sync.dma_start(
+                        out=w_raw[:, 2 * u : 2 * u + 2, :],
+                        in_=w[k0 : k0 + 2 * P, BLOCK * b : BLOCK * (b + 1)].rearrange("(q e) c -> q e c", e=2),
+                    )
+                pieces.append(w_raw)
+            return pieces
+
+        w_raws = [load_block(blocks[0][0], blocks[0][2])]
+        x_by_tile = x.rearrange("b (q j) c -> (b q) j c", j=TOKEN_TILES)
+        x_raws = []
+        for j in range(TOKEN_TILES):
+            x_raw = x_raw_pool.tile([P, C], BF16)
+            nc.sync.dma_start(out=x_raw[:], in_=x_by_tile[:, j, :])
+            x_raws.append(x_raw)
+        for w, out, b in blocks[1:]:
+            w_raws.append(load_block(w, b))
+
+        def new_block_tiles():
+            w_codes = w_mx.tile([P, PASSES, BLOCK], U32, align_bytes=64)
+            w_scales = w_mx.tile([P, PASSES, BLOCK], U8, align_bytes=64)
+            return {"codes": w_codes, "scales": w_scales, "grouped": []}
+
+        def regroup(mx, pieces, g):
+            w_grouped = w_stage.tile([P, BLOCK, PACK], BF16, align_bytes=64)
+            nc.vector.tensor_copy(
+                out=w_grouped[:].rearrange("p (c i) t -> p c t i", i=4),
+                in_=pieces[g][:].rearrange("p t (c i) -> p c t i", i=4),
+            )
+            mx["grouped"].append(w_grouped)
+
+        def quantise(mx, g):
+            nc.vector.quantize_mx(
+                out=mx["codes"][:, g, :].bitcast(FP8X4),
+                scales=mx["scales"][:, g, :],
+                in_=mx["grouped"][g][:].rearrange("p c t -> p (c t)"),
+            )
+
+        def prepare(mx, pieces, turn):
+            if turn < 2 * PASSES:
+                if turn % 2 == 0:
+                    regroup(mx, pieces, turn // 2)
+                else:
+                    quantise(mx, turn // 2)
+
+        w_next = new_block_tiles()
+        for turn in range(2 * PASSES):
+            prepare(w_next, w_raws[0], turn)
+
+        x_codes = const.tile([P, PASSES, TOKENS], U32, align_bytes=64)
+        x_scales = const.tile([P, PASSES, TOKENS], U8, align_bytes=64)
+        for j0 in range(0, TOKEN_TILES, 2):
+            for g in range(PASSES):
+                planes = psum.tile([P, 2, 2, P], F32, tag="bank")
+                for s in range(2):
+                    words = x_raws[j0 + s][:].bitcast(F32)
+                    for u in range(2):
+                        w0 = 2 * P * g + P * u
+                        nc.tensor.transpose(planes[:, s, u, :], words[:, w0 : w0 + P], ident[:])
+                x_grouped = x_stage.tile([P, 2 * P * PACK], BF16, align_bytes=64)
+                nc.scalar.copy(
+                    out=x_grouped[:].bitcast(F32).rearrange("p (s r u) -> p s r u", s=2, u=2),
+                    in_=planes[:].rearrange("p s u r -> p s r u"),
+                )
+                tokens = slice(P * j0, P * (j0 + 2))
+                nc.vector.quantize_mx(
+                    out=x_codes[:, g, tokens].bitcast(FP8X4),
+                    scales=x_scales[:, g, tokens],
+                    in_=x_grouped[:],
+                )
+
+        banks = {}
+
+        def products(step, mx, result):
+            j = step % TOKEN_TILES
+            tokens = slice(P * j, P * (j + 1))
+            acc = psum.tile([P, BLOCK], F32, tag="bank")
+            for g in range(PASSES):
+                nc.tensor.matmul_mx(
+                    out=acc[:],
+                    lhsT=x_codes[:, g, tokens].bitcast(FP8X4),
+                    lhsT_scale=x_scales[:, g, tokens],
+                    rhs=mx["codes"][:, g, :].bitcast(FP8X4),
+                    rhs_scale=mx["scales"][:, g, :],
+                    start=(g == 0),
+                    stop=(g == PASSES - 1),
+                )
+            banks[step] = {"acc": acc, "result": result}
+
+        def sums_of_squares(step):
+            acc = banks[step]["acc"]
+            squared = squares.tile([P, BLOCK], BF16)
+            sum_sq = norm.tile([P, BLOCK_HEADS], F32)
+            for h in range(BLOCK_HEADS):
+                cols = slice(DH * h, DH * (h + 1))
+                nc.scalar.activation(
+                    out=squared[:, cols], in_=acc[:, cols], func=ACT.Square, accum_out=sum_sq[:, h : h + 1]
+                )
+            banks[step]["sum_sq"] = sum_sq
+
+        def inverse_rms(step):
+            inv_rms = norm.tile([P, BLOCK_HEADS], F32)
+            nc.scalar.activation(
+                out=inv_rms[:], in_=banks[step]["sum_sq"][:], func=ACT.Abs_reciprocal_sqrt, scale=1.0 / DH, bias=EPS
+            )
+            banks[step]["inv_rms"] = inv_rms
+
+        def apply_norm(step):
+            j = step % TOKEN_TILES
+            acc, result, inv_rms = banks[step]["acc"], banks[step]["result"], banks[step]["inv_rms"]
+            if step % SCALAR_SCALES_EVERY == SCALAR_SCALES_EVERY - 1:
+                for h in range(BLOCK_HEADS):
+                    nc.scalar.activation(
+                        out=result[:, h, j, :],
+                        in_=acc[:, DH * h : DH * (h + 1)],
+                        func=ACT.Copy,
+                        scale=inv_rms[:, h : h + 1],
+                    )
+            else:
+                nc.vector.tensor_tensor(
+                    out=result[:, :, j, :],
+                    in0=acc[:].rearrange("p (h d) -> p h d", h=BLOCK_HEADS),
+                    in1=inv_rms[:].unsqueeze(2).to_broadcast([P, BLOCK_HEADS, DH]),
+                    op=ALU.mult,
+                )
+
+        def store(step):
+            j1 = step % TOKEN_TILES + 1
+            if j1 % STORE_TILES == 0:
+                w, out, b = blocks[step // TOKEN_TILES]
+                result = banks[step]["result"]
+                for h in range(BLOCK_HEADS):
+                    by_partition = out[:, BLOCK_HEADS * b + h, :, :].rearrange("b (q j) d -> b q j d", j=TOKEN_TILES)
+                    nc.sync.dma_start(
+                        out=by_partition[:, :, j1 - STORE_TILES : j1, :].rearrange("b q j d -> b q (j d)"),
+                        in_=result[:, h, j1 - STORE_TILES : j1, :].rearrange("p j d -> p (j d)"),
+                    )
+
+        steps = len(blocks) * TOKEN_TILES
+        for step in range(steps + SCALE_LAG):
+            n, j = step // TOKEN_TILES, step % TOKEN_TILES
+            if step < steps:
+                if j == 0:
+                    w_now = w_next
+                    if n + 1 < len(blocks):
+                        w_next = new_block_tiles()
+                    result = results.tile([P, BLOCK_HEADS, TOKEN_TILES, DH], F32)
+                products(step, w_now, result)
+                sums_of_squares(step)
+            if 1 <= step <= steps:
+                inverse_rms(step - 1)
+            if step >= SCALE_LAG:
+                apply_norm(step - SCALE_LAG)
+                store(step - SCALE_LAG)
+            if n + 1 < len(blocks):
+                prepare(w_next, w_raws[n + 1], j)

@@ -34,6 +34,7 @@ def tile_pieceroutedattention_pa_kernel(tc, x, Wq, Wk, out_0, out_1):
     blocks = [(w, out, b) for (w, out) in ((Wq, out_0), (Wk, out_1)) for b in range(BLOCKS_PER_WEIGHT)]
 
     with ExitStack() as ctx:
+        ctx.enter_context(tc.manual_schedule())
         const = ctx.enter_context(tc.tile_pool(name="const", bufs=1))
         x_raw_pool = ctx.enter_context(tc.tile_pool(name="x_raw", bufs=TOKEN_TILES))
         x_stage = ctx.enter_context(tc.tile_pool(name="x_stage", bufs=4))

@@ -22,55 +22,58 @@ BLOCK = 512
 BLOCK_HEADS = BLOCK // DH
 BLOCKS_PER_WEIGHT = HEADS * DH // BLOCK
 EPS = 2.0 ** -23
-SCALAR_SCALES_EVERY = 3
-STORE_TILES = 4
-SCALE_LAG = 2
+SCALAR_SCALES_EVERY = 4
+LAST_STORE_TILES = 2
+SCALE_LAG = 3
 
 FLOPS = 2 * TOKENS * C * 2 * HEADS * DH
 
 
 def tile_pieceroutedattention_pa_kernel(tc, x, Wq, Wk, out_0, out_1):
     nc = tc.nc
-    blocks = [(w, out, b) for (w, out) in ((Wq, out_0), (Wk, out_1)) for b in range(BLOCKS_PER_WEIGHT)]
+    blocks = [(out, b) for out in (out_0, out_1) for b in range(BLOCKS_PER_WEIGHT)]
 
     with ExitStack() as ctx:
-        ctx.enter_context(tc.manual_schedule())
         const = ctx.enter_context(tc.tile_pool(name="const", bufs=1))
-        x_raw_pool = ctx.enter_context(tc.tile_pool(name="x_raw", bufs=TOKEN_TILES))
+        x_raw_pool = ctx.enter_context(tc.tile_pool(name="x_raw", bufs=TOKEN_TILES // 2))
         x_stage = ctx.enter_context(tc.tile_pool(name="x_stage", bufs=4))
-        w_raw_pool = ctx.enter_context(tc.tile_pool(name="w_raw", bufs=len(blocks) * PASSES))
+        wq_raw_pool = ctx.enter_context(tc.tile_pool(name="wq_raw", bufs=BLOCKS_PER_WEIGHT * PASSES))
+        wk_raw_pool = ctx.enter_context(tc.tile_pool(name="wk_raw", bufs=PASSES))
         w_stage = ctx.enter_context(tc.tile_pool(name="w_stage", bufs=PASSES))
         w_mx = ctx.enter_context(tc.tile_pool(name="w_mx", bufs=2))
-        norm = ctx.enter_context(tc.tile_pool(name="norm", bufs=8))
+        norm = ctx.enter_context(tc.tile_pool(name="norm", bufs=4))
         squares = ctx.enter_context(tc.tile_pool(name="squares", bufs=4))
-        results = ctx.enter_context(tc.tile_pool(name="results", bufs=3))
+        results = ctx.enter_context(tc.tile_pool(name="results", bufs=4))
         psum = ctx.enter_context(tc.psum_pool(name="psum", bufs=8))
 
         ident = const.tile([P, P], F32)
         make_identity(nc, ident[:])
 
-        def load_block(w, b):
-            pieces = []
-            for g in range(PASSES):
-                w_raw = w_raw_pool.tile([P, PACK, BLOCK], BF16)
-                for u in range(2):
-                    k0 = K_PASS * g + 2 * P * u
-                    nc.sync.dma_start(
-                        out=w_raw[:, 2 * u : 2 * u + 2, :],
-                        in_=w[k0 : k0 + 2 * P, BLOCK * b : BLOCK * (b + 1)].rearrange("(q e) c -> q e c", e=2),
-                    )
-                pieces.append(w_raw)
-            return pieces
+        def load_pass(pool, w, g, c0, width):
+            w_raw = pool.tile([P, PACK, width], BF16)
+            for u in range(2):
+                k0 = K_PASS * g + 2 * P * u
+                nc.sync.dma_start(
+                    out=w_raw[:, 2 * u : 2 * u + 2, :],
+                    in_=w[k0 : k0 + 2 * P, c0 : c0 + width].rearrange("(q e) c -> q e c", e=2),
+                )
+            return w_raw
 
-        w_raws = [load_block(blocks[0][0], blocks[0][2])]
+        def load_wq_block(b):
+            return [load_pass(wq_raw_pool, Wq, g, BLOCK * b, BLOCK)[:] for g in range(PASSES)]
+
+        w_raws = [load_wq_block(0)]
         x_by_tile = x.rearrange("b (q j) c -> (b q) j c", j=TOKEN_TILES)
         x_raws = []
-        for j in range(TOKEN_TILES):
-            x_raw = x_raw_pool.tile([P, C], BF16)
-            nc.sync.dma_start(out=x_raw[:], in_=x_by_tile[:, j, :])
+        for j0 in range(0, TOKEN_TILES, 2):
+            x_raw = x_raw_pool.tile([P, 2, C], BF16)
+            nc.sync.dma_start(out=x_raw[:], in_=x_by_tile[:, j0 : j0 + 2, :])
             x_raws.append(x_raw)
-        for w, out, b in blocks[1:]:
-            w_raws.append(load_block(w, b))
+        for b in range(1, BLOCKS_PER_WEIGHT):
+            w_raws.append(load_wq_block(b))
+        wk_raws = [load_pass(wk_raw_pool, Wk, g, 0, HEADS * DH) for g in range(PASSES)]
+        for b in range(BLOCKS_PER_WEIGHT):
+            w_raws.append([wk_raw[:, :, BLOCK * b : BLOCK * (b + 1)] for wk_raw in wk_raws])
 
         def new_block_tiles():
             w_codes = w_mx.tile([P, PASSES, BLOCK], U32, align_bytes=64)
@@ -81,7 +84,7 @@ def tile_pieceroutedattention_pa_kernel(tc, x, Wq, Wk, out_0, out_1):
             w_grouped = w_stage.tile([P, BLOCK, PACK], BF16, align_bytes=64)
             nc.vector.tensor_copy(
                 out=w_grouped[:].rearrange("p (c i) t -> p c t i", i=4),
-                in_=pieces[g][:].rearrange("p t (c i) -> p c t i", i=4),
+                in_=pieces[g].rearrange("p t (c i) -> p c t i", i=4),
             )
             mx["grouped"].append(w_grouped)
 
@@ -105,20 +108,21 @@ def tile_pieceroutedattention_pa_kernel(tc, x, Wq, Wk, out_0, out_1):
 
         x_codes = const.tile([P, PASSES, TOKENS], U32, align_bytes=64)
         x_scales = const.tile([P, PASSES, TOKENS], U8, align_bytes=64)
-        for j0 in range(0, TOKEN_TILES, 2):
+        for pair, x_raw in enumerate(x_raws):
             for g in range(PASSES):
                 planes = psum.tile([P, 2, 2, P], F32, tag="bank")
                 for s in range(2):
-                    words = x_raws[j0 + s][:].bitcast(F32)
+                    words = x_raw[:, s, :].bitcast(F32)
                     for u in range(2):
                         w0 = 2 * P * g + P * u
                         nc.tensor.transpose(planes[:, s, u, :], words[:, w0 : w0 + P], ident[:])
                 x_grouped = x_stage.tile([P, 2 * P * PACK], BF16, align_bytes=64)
-                nc.scalar.copy(
-                    out=x_grouped[:].bitcast(F32).rearrange("p (s r u) -> p s r u", s=2, u=2),
-                    in_=planes[:].rearrange("p s u r -> p s r u"),
-                )
-                tokens = slice(P * j0, P * (j0 + 2))
+                side_by_side = x_grouped[:].bitcast(F32).rearrange("p (s r u) -> p s r u", s=2, u=2)
+                if g == 2:
+                    nc.vector.tensor_copy(out=side_by_side, in_=planes[:].rearrange("p s u r -> p s r u"))
+                else:
+                    nc.scalar.copy(out=side_by_side, in_=planes[:].rearrange("p s u r -> p s r u"))
+                tokens = slice(2 * P * pair, 2 * P * (pair + 1))
                 nc.vector.quantize_mx(
                     out=x_codes[:, g, tokens].bitcast(FP8X4),
                     scales=x_scales[:, g, tokens],
@@ -144,26 +148,36 @@ def tile_pieceroutedattention_pa_kernel(tc, x, Wq, Wk, out_0, out_1):
             banks[step] = {"acc": acc, "result": result}
 
         def sums_of_squares(step):
+            if step % 2 == 0:
+                sum_sq = norm.tile([P, 2, BLOCK_HEADS], F32)
+                inv_rms = norm.tile([P, 2, BLOCK_HEADS], F32)
+                banks[step].update({"sum_sq": sum_sq, "inv_rms": inv_rms})
+            else:
+                banks[step].update({"sum_sq": banks[step - 1]["sum_sq"], "inv_rms": banks[step - 1]["inv_rms"]})
             acc = banks[step]["acc"]
             squared = squares.tile([P, BLOCK], BF16)
-            sum_sq = norm.tile([P, BLOCK_HEADS], F32)
             for h in range(BLOCK_HEADS):
                 cols = slice(DH * h, DH * (h + 1))
                 nc.scalar.activation(
-                    out=squared[:, cols], in_=acc[:, cols], func=ACT.Square, accum_out=sum_sq[:, h : h + 1]
+                    out=squared[:, cols],
+                    in_=acc[:, cols],
+                    func=ACT.Square,
+                    accum_out=banks[step]["sum_sq"][:, step % 2, h : h + 1],
                 )
-            banks[step]["sum_sq"] = sum_sq
 
         def inverse_rms(step):
-            inv_rms = norm.tile([P, BLOCK_HEADS], F32)
             nc.scalar.activation(
-                out=inv_rms[:], in_=banks[step]["sum_sq"][:], func=ACT.Abs_reciprocal_sqrt, scale=1.0 / DH, bias=EPS
+                out=banks[step]["inv_rms"][:],
+                in_=banks[step]["sum_sq"][:],
+                func=ACT.Abs_reciprocal_sqrt,
+                scale=1.0 / DH,
+                bias=EPS,
             )
-            banks[step]["inv_rms"] = inv_rms
 
         def apply_norm(step):
             j = step % TOKEN_TILES
-            acc, result, inv_rms = banks[step]["acc"], banks[step]["result"], banks[step]["inv_rms"]
+            acc, result = banks[step]["acc"], banks[step]["result"]
+            inv_rms = banks[step]["inv_rms"][:, step % 2, :]
             if step % SCALAR_SCALES_EVERY == SCALAR_SCALES_EVERY - 1:
                 for h in range(BLOCK_HEADS):
                     nc.scalar.activation(
@@ -176,20 +190,21 @@ def tile_pieceroutedattention_pa_kernel(tc, x, Wq, Wk, out_0, out_1):
                 nc.vector.tensor_tensor(
                     out=result[:, :, j, :],
                     in0=acc[:].rearrange("p (h d) -> p h d", h=BLOCK_HEADS),
-                    in1=inv_rms[:].unsqueeze(2).to_broadcast([P, BLOCK_HEADS, DH]),
+                    in1=inv_rms.unsqueeze(2).to_broadcast([P, BLOCK_HEADS, DH]),
                     op=ALU.mult,
                 )
 
         def store(step):
-            j1 = step % TOKEN_TILES + 1
-            if j1 % STORE_TILES == 0:
-                w, out, b = blocks[step // TOKEN_TILES]
+            n, j1 = step // TOKEN_TILES, step % TOKEN_TILES + 1
+            group = LAST_STORE_TILES if n == len(blocks) - 1 else TOKEN_TILES
+            if j1 % group == 0:
+                out, b = blocks[n]
                 result = banks[step]["result"]
                 for h in range(BLOCK_HEADS):
                     by_partition = out[:, BLOCK_HEADS * b + h, :, :].rearrange("b (q j) d -> b q j d", j=TOKEN_TILES)
                     nc.sync.dma_start(
-                        out=by_partition[:, :, j1 - STORE_TILES : j1, :].rearrange("b q j d -> b q (j d)"),
-                        in_=result[:, h, j1 - STORE_TILES : j1, :].rearrange("p j d -> p (j d)"),
+                        out=by_partition[:, :, j1 - group : j1, :].rearrange("b q j d -> b q (j d)"),
+                        in_=result[:, h, j1 - group : j1, :].rearrange("p j d -> p (j d)"),
                     )
 
         steps = len(blocks) * TOKEN_TILES
@@ -203,7 +218,7 @@ def tile_pieceroutedattention_pa_kernel(tc, x, Wq, Wk, out_0, out_1):
                     result = results.tile([P, BLOCK_HEADS, TOKEN_TILES, DH], F32)
                 products(step, w_now, result)
                 sums_of_squares(step)
-            if 1 <= step <= steps:
+            if step % 2 == 0 and 2 <= step <= steps:
                 inverse_rms(step - 1)
             if step >= SCALE_LAG:
                 apply_norm(step - SCALE_LAG)

from contextlib import ExitStack

import concourse.mybir as mybir
from concourse.masks import make_identity

F32 = mybir.dt.float32
BF16 = mybir.dt.bfloat16
U32 = mybir.dt.uint32
U8 = mybir.dt.uint8
FP8X4 = mybir.dt.float8_e4m3fn_x4
ACT = mybir.ActivationFunctionType
ALU = mybir.AluOpType

P = 128
PACK = 4
K_PASS = P * PACK
BOARDS, SQUARES, C, HEADS, DH = 16, 64, 1536, 12, 128
TOKENS = BOARDS * SQUARES
TOKEN_TILES = TOKENS // P
PASSES = C // K_PASS
BLOCK = 512
BLOCK_HEADS = BLOCK // DH
BLOCKS_PER_WEIGHT = HEADS * DH // BLOCK
EPS = 2.0 ** -23
SCALAR_SCALES_EVERY = 4
LAST_STORE_TILES = 2
SCALE_LAG = 3

FLOPS = 2 * TOKENS * C * 2 * HEADS * DH


def tile_pieceroutedattention_pa_kernel(tc, x, Wq, Wk, out_0, out_1):
    nc = tc.nc
    blocks = [(out, b) for out in (out_0, out_1) for b in range(BLOCKS_PER_WEIGHT)]

    with ExitStack() as ctx:
        const = ctx.enter_context(tc.tile_pool(name="const", bufs=1))
        x_raw_pool = ctx.enter_context(tc.tile_pool(name="x_raw", bufs=TOKEN_TILES // 2))
        x_stage = ctx.enter_context(tc.tile_pool(name="x_stage", bufs=4))
        wq_raw_pool = ctx.enter_context(tc.tile_pool(name="wq_raw", bufs=BLOCKS_PER_WEIGHT * PASSES))
        wk_raw_pool = ctx.enter_context(tc.tile_pool(name="wk_raw", bufs=PASSES))
        w_stage = ctx.enter_context(tc.tile_pool(name="w_stage", bufs=PASSES))
        w_mx = ctx.enter_context(tc.tile_pool(name="w_mx", bufs=2))
        norm = ctx.enter_context(tc.tile_pool(name="norm", bufs=4))
        squares = ctx.enter_context(tc.tile_pool(name="squares", bufs=4))
        results = ctx.enter_context(tc.tile_pool(name="results", bufs=4))
        psum = ctx.enter_context(tc.psum_pool(name="psum", bufs=8))

        ident = const.tile([P, P], F32)
        make_identity(nc, ident[:])

        def load_pass(pool, w, g, c0, width):
            w_raw = pool.tile([P, PACK, width], BF16)
            for u in range(2):
                k0 = K_PASS * g + 2 * P * u
                nc.sync.dma_start(
                    out=w_raw[:, 2 * u : 2 * u + 2, :],
                    in_=w[k0 : k0 + 2 * P, c0 : c0 + width].rearrange("(q e) c -> q e c", e=2),
                )
            return w_raw

        def load_wq_block(b):
            return [load_pass(wq_raw_pool, Wq, g, BLOCK * b, BLOCK)[:] for g in range(PASSES)]

        w_raws = [load_wq_block(0)]
        x_by_tile = x.rearrange("b (q j) c -> (b q) j c", j=TOKEN_TILES)
        x_raws = []
        for j0 in range(0, TOKEN_TILES, 2):
            x_raw = x_raw_pool.tile([P, 2, C], BF16)
            nc.sync.dma_start(out=x_raw[:], in_=x_by_tile[:, j0 : j0 + 2, :])
            x_raws.append(x_raw)
        for b in range(1, BLOCKS_PER_WEIGHT):
            w_raws.append(load_wq_block(b))
        wk_raws = [load_pass(wk_raw_pool, Wk, g, 0, HEADS * DH) for g in range(PASSES)]
        for b in range(BLOCKS_PER_WEIGHT):
            w_raws.append([wk_raw[:, :, BLOCK * b : BLOCK * (b + 1)] for wk_raw in wk_raws])

        def new_block_tiles():
            w_codes = w_mx.tile([P, PASSES, BLOCK], U32, align_bytes=64)
            w_scales = w_mx.tile([P, PASSES, BLOCK], U8, align_bytes=64)
            return {"codes": w_codes, "scales": w_scales, "grouped": []}

        def regroup(mx, pieces, g):
            w_grouped = w_stage.tile([P, BLOCK, PACK], BF16, align_bytes=64)
            nc.vector.tensor_copy(
                out=w_grouped[:].rearrange("p (c i) t -> p c t i", i=4),
                in_=pieces[g].rearrange("p t (c i) -> p c t i", i=4),
            )
            mx["grouped"].append(w_grouped)

        def quantise(mx, g):
            nc.vector.quantize_mx(
                out=mx["codes"][:, g, :].bitcast(FP8X4),
                scales=mx["scales"][:, g, :],
                in_=mx["grouped"][g][:].rearrange("p c t -> p (c t)"),
            )

        def prepare(mx, pieces, turn):
            if turn < 2 * PASSES:
                if turn % 2 == 0:
                    regroup(mx, pieces, turn // 2)
                else:
                    quantise(mx, turn // 2)

        w_next = new_block_tiles()
        for turn in range(2 * PASSES):
            prepare(w_next, w_raws[0], turn)

        x_codes = const.tile([P, PASSES, TOKENS], U32, align_bytes=64)
        x_scales = const.tile([P, PASSES, TOKENS], U8, align_bytes=64)
        for pair, x_raw in enumerate(x_raws):
            for g in range(PASSES):
                planes = psum.tile([P, 2, 2, P], F32, tag="bank")
                for s in range(2):
                    words = x_raw[:, s, :].bitcast(F32)
                    for u in range(2):
                        w0 = 2 * P * g + P * u
                        nc.tensor.transpose(planes[:, s, u, :], words[:, w0 : w0 + P], ident[:])
                x_grouped = x_stage.tile([P, 2 * P * PACK], BF16, align_bytes=64)
                side_by_side = x_grouped[:].bitcast(F32).rearrange("p (s r u) -> p s r u", s=2, u=2)
                if g == 2:
                    nc.vector.tensor_copy(out=side_by_side, in_=planes[:].rearrange("p s u r -> p s r u"))
                else:
                    nc.scalar.copy(out=side_by_side, in_=planes[:].rearrange("p s u r -> p s r u"))
                tokens = slice(2 * P * pair, 2 * P * (pair + 1))
                nc.vector.quantize_mx(
                    out=x_codes[:, g, tokens].bitcast(FP8X4),
                    scales=x_scales[:, g, tokens],
                    in_=x_grouped[:],
                )

        banks = {}

        def products(step, mx, result):
            j = step % TOKEN_TILES
            tokens = slice(P * j, P * (j + 1))
            acc = psum.tile([P, BLOCK], F32, tag="bank")
            for g in range(PASSES):
                nc.tensor.matmul_mx(
                    out=acc[:],
                    lhsT=x_codes[:, g, tokens].bitcast(FP8X4),
                    lhsT_scale=x_scales[:, g, tokens],
                    rhs=mx["codes"][:, g, :].bitcast(FP8X4),
                    rhs_scale=mx["scales"][:, g, :],
                    start=(g == 0),
                    stop=(g == PASSES - 1),
                )
            banks[step] = {"acc": acc, "result": result}

        def sums_of_squares(step):
            if step % 2 == 0:
                sum_sq = norm.tile([P, 2, BLOCK_HEADS], F32)
                inv_rms = norm.tile([P, 2, BLOCK_HEADS], F32)
                banks[step].update({"sum_sq": sum_sq, "inv_rms": inv_rms})
            else:
                banks[step].update({"sum_sq": banks[step - 1]["sum_sq"], "inv_rms": banks[step - 1]["inv_rms"]})
            acc = banks[step]["acc"]
            squared = squares.tile([P, BLOCK], BF16)
            for h in range(BLOCK_HEADS):
                cols = slice(DH * h, DH * (h + 1))
                nc.scalar.activation(
                    out=squared[:, cols],
                    in_=acc[:, cols],
                    func=ACT.Square,
                    accum_out=banks[step]["sum_sq"][:, step % 2, h : h + 1],
                )

        def inverse_rms(step):
            nc.scalar.activation(
                out=banks[step]["inv_rms"][:],
                in_=banks[step]["sum_sq"][:],
                func=ACT.Abs_reciprocal_sqrt,
                scale=1.0 / DH,
                bias=EPS,
            )

        def apply_norm(step):
            j = step % TOKEN_TILES
            acc, result = banks[step]["acc"], banks[step]["result"]
            inv_rms = banks[step]["inv_rms"][:, step % 2, :]
            if step % SCALAR_SCALES_EVERY == SCALAR_SCALES_EVERY - 1:
                for h in range(BLOCK_HEADS):
                    nc.scalar.activation(
                        out=result[:, h, j, :],
                        in_=acc[:, DH * h : DH * (h + 1)],
                        func=ACT.Copy,
                        scale=inv_rms[:, h : h + 1],
                    )
            else:
                nc.vector.tensor_tensor(
                    out=result[:, :, j, :],
                    in0=acc[:].rearrange("p (h d) -> p h d", h=BLOCK_HEADS),
                    in1=inv_rms.unsqueeze(2).to_broadcast([P, BLOCK_HEADS, DH]),
                    op=ALU.mult,
                )

        def store(step):
            n, j1 = step // TOKEN_TILES, step % TOKEN_TILES + 1
            group = LAST_STORE_TILES if n == len(blocks) - 1 else TOKEN_TILES
            if j1 % group == 0:
                out, b = blocks[n]
                result = banks[step]["result"]
                for h in range(BLOCK_HEADS):
                    by_partition = out[:, BLOCK_HEADS * b + h, :, :].rearrange("b (q j) d -> b q j d", j=TOKEN_TILES)
                    nc.sync.dma_start(
                        out=by_partition[:, :, j1 - group : j1, :].rearrange("b q j d -> b q (j d)"),
                        in_=result[:, h, j1 - group : j1, :].rearrange("p j d -> p (j d)"),
                    )

        steps = len(blocks) * TOKEN_TILES
        for step in range(steps + SCALE_LAG):
            n, j = step // TOKEN_TILES, step % TOKEN_TILES
            if step < steps:
                if j == 0:
                    w_now = w_next
                    if n + 1 < len(blocks):
                        w_next = new_block_tiles()
                    result = results.tile([P, BLOCK_HEADS, TOKEN_TILES, DH], F32)
                products(step, w_now, result)
                sums_of_squares(step)
            if step % 2 == 0 and 2 <= step <= steps:
                inverse_rms(step - 1)
            if step >= SCALE_LAG:
                apply_norm(step - SCALE_LAG)
                store(step - SCALE_LAG)
            if n + 1 < len(blocks):
                prepare(w_next, w_raws[n + 1], j)
